import numpy as np
import ml_dtypes


def mxq(x, axis, fmt="e4m3"):
    dtype, down = {"e4m3": (ml_dtypes.float8_e4m3fn, 7), "e5m2": (ml_dtypes.float8_e5m2, 14)}[fmt]
    v = np.moveaxis(np.asarray(x, np.float32).astype(ml_dtypes.bfloat16).astype(np.float64), axis, -1)
    blocks = v.reshape(v.shape[:-1] + (-1, 32))
    amax = np.abs(blocks).max(-1, keepdims=True)
    byte = np.maximum(np.where(amax > 0, np.frexp(amax)[1] - 1 + 127, 0) - down, 1)
    scale = np.exp2(byte - 127.0)
    codes = (blocks / scale).astype(np.float32).astype(dtype).astype(np.float64)
    return np.moveaxis((codes * scale).reshape(v.shape), -1, axis)


WIDE = False


def mx_kscale(k):
    if not WIDE:
        return np.ones(k)
    levels = np.array([10, -10, 5, -5, 0])
    if k % 512:
        return np.exp2(np.random.permutation(np.resize(levels, k // 32))).repeat(32)
    a = np.empty((k // 512, 16))
    for p in range(k // 512):
        a[p, :8] = np.random.permutation(np.resize(levels, 8))
        for g in range(8):
            far = levels[np.abs(levels - a[p, g]) >= 10]
            a[p, g + 8] = far[np.random.randint(len(far))]
    return np.exp2(a.ravel()).repeat(32)


BF16 = ml_dtypes.bfloat16


def bf(x):
    return np.asarray(x, np.float32).astype(BF16)


def f64(x):
    return np.asarray(x).astype(np.float64)


B, C, H, W, O, KH, KW, PH, PW, T, R = 4, 1024, 7, 7, 512, 2, 2, 1, 1, 8, 64
HO, WO = H + PH + PH - KH + 1, W + PW + PW - KW + 1
N = B * HO * WO
D = C * KH * KW
R2 = R * KH * KW
K1, K2 = T * R, T * R2


def setup_inputs():
    s, t1, t2 = mx_kscale(D), mx_kscale(K1).reshape(T, R), mx_kscale(K2).reshape(T, R2)
    return {"xw": bf(np.random.standard_normal((N, D)) * s),
            "S1s": bf(np.random.standard_normal((T, D, R)) / np.sqrt(D) / s[None, :, None] * t1[:, None, :]),
            "U1s": bf(np.random.standard_normal((T, R, O)) * T / np.sqrt(K1) / t1[:, :, None]),
            "U2s": bf(np.random.standard_normal((T, R2, D)) / np.sqrt(D) / s[None, None, :] * t2[:, :, None]),
            "S2s": bf(np.random.standard_normal((T, R2, O)) * T / np.sqrt(K2) / t2[:, :, None]),
            "bias": bf(np.random.standard_normal(O) * 0.3)}


def reference(xw, S1s, U1s, U2s, S2s, bias):
    xq = mxq(f64(xw), 1, "e4m3")
    s1 = f64(S1s).transpose(1, 0, 2).reshape(D, K1)
    h1 = xq @ mxq(s1, 0, "e4m3")
    out1 = (mxq(h1, 1, "e4m3") @ mxq(f64(U1s).reshape(K1, O), 0, "e4m3")) / T + f64(bias)
    u2 = f64(U2s).reshape(K2, D)
    h2 = xq @ mxq(u2, 1, "e4m3").T
    out2 = (mxq(h2, 1, "e4m3") @ mxq(f64(S2s).reshape(K2, O), 0, "e4m3")) / T
    out = out1 + out2 + f64(bias)
    return out.reshape(B, HO, WO, O).transpose(0, 3, 1, 2)

@@ -1,0 +1,294 @@
+from contextlib import ExitStack
+
+import concourse.mybir as mybir
+from concourse.masks import make_identity
+
+PIN = True
+
+FLOPS = 2 * 256 * 4096 * (512 + 2048) + 2 * 256 * 512 * (512 + 2048)
+
+BF16 = mybir.dt.bfloat16
+F32 = mybir.dt.float32
+U32 = mybir.dt.uint32
+U8 = mybir.dt.uint8
+FP8X4 = mybir.dt.float8_e4m3fn_x4
+ACT = mybir.ActivationFunctionType
+ALU = mybir.AluOpType
+
+P = 128
+NW = 256
+D = 4096
+NC = 8
+HALF = 2048
+
+
+def tile_skconv2d_pa_kernel(tc, xw, S1s, U1s, U2s, S2s, bias, out):
+    nc = tc.nc
+    u2v = U2s.rearrange("t r k -> (t r) k").rearrange("(g p j) k -> p g j k", p=P, j=4)
+    s1v = S1s.rearrange("t (c p e) r -> p t c (e r)", c=NC, p=P, e=4)
+    u1v = U1s.rearrange("t r o -> (t r) o").rearrange("(p j) o -> p j o", p=P)
+    s2v = S2s.rearrange("t r o -> (t r) o").rearrange("(g p j) o -> p g j o", p=P, j=4)
+    outv = out.rearrange("b (q p) i j -> p q b (i j)", p=P)
+
+    with ExitStack() as ctx:
+        const = ctx.enter_context(tc.tile_pool(name="const", bufs=1))
+        rawp = ctx.enter_context(tc.tile_pool(name="rawp", bufs=8))
+        grpp = ctx.enter_context(tc.tile_pool(name="grpp", bufs=3))
+        codp = ctx.enter_context(tc.tile_pool(name="codp", bufs=3))
+        s1gp = ctx.enter_context(tc.tile_pool(name="s1gp", bufs=4))
+        s1cp = ctx.enter_context(tc.tile_pool(name="s1cp", bufs=4))
+        wgp = ctx.enter_context(tc.tile_pool(name="wgp", bufs=2))
+        hgp = ctx.enter_context(tc.tile_pool(name="hgp", bufs=2))
+        tps = ctx.enter_context(tc.psum_pool(name="tps", bufs=6))
+        hps = ctx.enter_context(tc.psum_pool(name="hps", bufs=2))
+        if PIN:
+            ctx.enter_context(tc.manual_schedule())
+
+        ident_f = const.tile([P, P], F32, name="ident_f")
+        make_identity(nc, ident_f[:])
+        ident_b = const.tile([P, P], BF16, name="ident_b")
+        make_identity(nc, ident_b[:])
+        bz = const.tile([P, P], BF16, name="bz")
+        nc.vector.memset(bz[:], 0.0)
+        nc.scalar.dma_start(out=bz[0:4, :], in_=bias.rearrange("(a c) -> a c", a=4))
+
+        xq = const.tile([P, NC, NW], U32, name="xq", align_bytes=64)
+        xs = const.tile([P, NC, NW], U8, name="xs", align_bytes=64)
+        s2r = const.tile([P, 4, 4, 512], BF16, name="s2r")
+        u1r = const.tile([P, 4, 512], BF16, name="u1r")
+        wc = const.tile([P, 5, 512], U32, name="wc", align_bytes=64)
+        ws = const.tile([P, 5, 512], U8, name="ws", align_bytes=64)
+        hqc = const.tile([P, 5, NW], U32, name="hqc", align_bytes=64)
+        hqs = const.tile([P, 5, NW], U8, name="hqs", align_bytes=64)
+        osb = const.tile([P, 4, NW], F32, name="osb")
+        b2 = const.tile([P, 4], F32, name="b2")
+
+        xr = [rawp.tile([P, D], BF16, name="xr%d" % a, tag="raw") for a in range(2)]
+        for hf in range(2):
+            for a in range(2):
+                nc.sync.dma_start(
+                    out=xr[a][:, HALF * hf : HALF * (hf + 1)],
+                    in_=xw[P * a : P * (a + 1), HALF * hf : HALF * (hf + 1)],
+                )
+        u2raw = {}
+        s1raw = {}
+
+        def load_raw(n):
+            if n < 16:
+                t = rawp.tile([P, D], BF16, name="u2r", tag="raw")
+                nc.sync.dma_start(out=t[:], in_=u2v[:, n // 4, n % 4, :])
+                u2raw[n] = t
+            elif n < 20:
+                m = n - 16
+                t = rawp.tile([P, D], BF16, name="s1r", tag="raw")
+                for t2 in range(2):
+                    nc.sync.dma_start(
+                        out=t[:, HALF * t2 : HALF * (t2 + 1)].rearrange("p (c x) -> p c x", c=NC),
+                        in_=s1v[:, 2 * m + t2],
+                    )
+                s1raw[m] = t
+            if n == 3:
+                nc.sync.dma_start(out=u1r[:], in_=u1v)
+            if n in (5, 7, 9, 11):
+                g = (n - 5) // 2
+                nc.sync.dma_start(out=s2r[:, g], in_=s2v[:, g])
+
+        for n in range(6):
+            load_raw(n)
+
+        def quant(codes, scales, src):
+            nc.vector.quantize_mx(out=codes.bitcast(FP8X4), scales=scales, in_=src)
+
+        xg = []
+
+        def quant_x(k):
+            quant(
+                xq[:, 2 * k : 2 * k + 2, :].rearrange("p c n -> p (c n)"),
+                xs[:, 2 * k : 2 * k + 2, :].rearrange("p c n -> p (c n)"),
+                xg[k // 2][:, 2 * (k % 2) : 2 * (k % 2) + 2].rearrange("p c n t -> p (c n t)"),
+            )
+
+        for c in range(NC):
+            if c % 4 == 0:
+                xg.append(grpp.tile([P, 4, NW, 4], BF16, name="xg", tag="grp", align_bytes=64))
+            gf = xg[c // 4][:].bitcast(F32)
+            bank = tps.tile([P, 2, NW], F32, name="xb", tag="T")
+            for u in range(2):
+                for a in range(2):
+                    nc.tensor.transpose(
+                        bank[:, u, P * a : P * (a + 1)],
+                        xr[a][:].bitcast(F32)[:, 256 * c + u : 256 * (c + 1) : 2],
+                        ident_f[:],
+                    )
+            src = bank[:].rearrange("p u n -> p n u")
+            if c % 2 == 0:
+                nc.vector.tensor_copy(out=gf[:, c % 4], in_=src)
+            else:
+                nc.scalar.copy(out=gf[:, c % 4], in_=src)
+            if c % 2 == 0 and c >= 2:
+                quant_x(c // 2 - 1)
+        quant_x(3)
+        load_raw(6)
+        load_raw(7)
+
+        bt = tps.tile([P, P], BF16, name="bt", tag="T")
+        nc.tensor.transpose(bt[:], bz[:], ident_b[:])
+        nc.scalar.mul(b2[:], bt[:, 0:4], 2.0)
+
+        u2grp = {}
+        u2cod = {}
+        hbank = {}
+        hgrp = {}
+
+        def transposes(i):
+            grp = grpp.tile([P, NC, P, 4], BF16, name="u2g", tag="grp", align_bytes=64)
+            u2grp[i] = grp
+            gf = grp[:].bitcast(F32)
+            rf = u2raw[i][:].bitcast(F32)
+            for b in range(4):
+                bank = tps.tile([P, 2, 2, P], F32, name="ub", tag="T")
+                for c2 in range(2):
+                    for u in range(2):
+                        c = 2 * b + c2
+                        nc.tensor.transpose(
+                            bank[:, c2, u, :], rf[:, 256 * c + u : 256 * (c + 1) : 2], ident_f[:]
+                        )
+                src = bank[:].rearrange("p c u r -> p c r u")
+                if b == 0 and i % 2 == 1:
+                    nc.vector.tensor_copy(out=gf[:, 2 * b : 2 * b + 2], in_=src)
+                else:
+                    nc.scalar.copy(out=gf[:, 2 * b : 2 * b + 2], in_=src)
+            load_raw(8 + i)
+
+        def quant_u2(i):
+            cod = codp.tile([P, NC, P], U32, name="u2c", tag="u2c", align_bytes=64)
+            scl = codp.tile([P, NC, P], U8, name="u2s", tag="u2s", align_bytes=64)
+            u2cod[i] = (cod, scl)
+            for hf in range(2):
+                sl = slice(4 * hf, 4 * hf + 4)
+                quant(
+                    cod[:, sl, :].rearrange("p c r -> p (c r)"),
+                    scl[:, sl, :].rearrange("p c r -> p (c r)"),
+                    u2grp[i][:, sl].rearrange("p c r t -> p (c r t)"),
+                )
+
+        def first_stage(key, half, cod, scl):
+            if half == 0:
+                hbank[key] = hps.tile([P, 2, NW], F32, name="hb", tag="h")
+            hb = hbank[key]
+            for c in range(NC):
+                nc.tensor.matmul_mx(
+                    out=hb[:, half, :],
+                    lhsT=cod[:, c, :].bitcast(FP8X4),
+                    lhsT_scale=scl[:, c, :],
+                    rhs=xq[:, c, :].bitcast(FP8X4),
+                    rhs_scale=xs[:, c, :],
+                    start=(c == 0),
+                    stop=(c == NC - 1),
+                )
+
+        def h_copy(s, pair, key):
+            if pair == 0:
+                hgrp[s] = hgp.tile([P, NW, 4], BF16, name="hg", tag="hg", align_bytes=64)
+            nc.scalar.copy(
+                out=hgrp[s][:, :, 2 * pair : 2 * pair + 2],
+                in_=hbank[key][:].rearrange("p j n -> p n j"),
+            )
+
+        def h_quant(s):
+            quant(hqc[:, s, :], hqs[:, s, :], hgrp[s][:].rearrange("p n t -> p (n t)"))
+
+        wgrp = {}
+
+        def w_regroup(s):
+            wg = wgp.tile([P, 512, 4], BF16, name="wg", tag="wg", align_bytes=64)
+            wgrp[s] = wg
+            src = u1r[:] if s == 4 else s2r[:, s]
+            nc.vector.tensor_copy(
+                out=wg[:].rearrange("p (c i) t -> p c t i", i=4),
+                in_=src.rearrange("p t (c i) -> p c t i", i=4),
+            )
+
+        def w_quant(s):
+            quant(wc[:, s, :], ws[:, s, :], wgrp[s][:].rearrange("p o t -> p (o t)"))
+
+        w_order = {4: 4, 6: 0, 8: 1, 10: 2, 12: 3}
+
+        transposes(0)
+        quant_u2(0)
+        transposes(1)
+        quant_u2(1)
+        for i in range(16):
+            g, j = i // 4, i % 4
+            first_stage(("u2", i // 2), j % 2, u2cod[i][0], u2cod[i][1])
+            if i + 2 < 16:
+                transposes(i + 2)
+            if j % 2 == 1:
+                h_copy(g, j // 2, ("u2", i // 2))
+            if i + 2 < 16:
+                quant_u2(i + 2)
+            if j == 3:
+                h_quant(g)
+            if i in w_order:
+                w_regroup(w_order[i])
+            if i - 1 in w_order:
+                w_quant(w_order[i - 1])
+
+        acc = [tps.tile([P, 512], F32, name="acc%d" % q, tag="T") for q in range(4)]
+
+        def second_stage(s, start, stop):
+            for q in range(4):
+                nc.tensor.matmul_mx(
+                    out=acc[q][:, 0:NW],
+                    lhsT=wc[:, s, P * q : P * (q + 1)].bitcast(FP8X4),
+                    lhsT_scale=ws[:, s, P * q : P * (q + 1)],
+                    rhs=hqc[:, s, :].bitcast(FP8X4),
+                    rhs_scale=hqs[:, s, :],
+                    start=start,
+                    stop=stop,
+                )
+
+        for g in range(4):
+            second_stage(g, g == 0, False)
+
+        s1g = [
+            s1gp.tile([P, NC, 8, 16, 4], BF16, name="s1g%d" % j, tag="s1g", align_bytes=64)
+            for j in range(4)
+        ]
+        for t in range(8):
+            src = s1raw[t // 2][:, HALF * (t % 2) : HALF * (t % 2 + 1)].rearrange(
+                "p (c e r j) -> p c j r e", c=NC, e=4, r=16, j=4
+            )
+            for j in range(4):
+                if j % 2 == 0:
+                    nc.vector.tensor_copy(out=s1g[j][:, :, t], in_=src[:, :, j])
+                else:
+                    nc.scalar.copy(out=s1g[j][:, :, t], in_=src[:, :, j])
+        for j in range(4):
+            cod = s1cp.tile([P, NC, P], U32, name="s1c", tag="s1c", align_bytes=64)
+            scl = s1cp.tile([P, NC, P], U8, name="s1s", tag="s1s", align_bytes=64)
+            for hf in range(2):
+                sl = slice(4 * hf, 4 * hf + 4)
+                quant(
+                    cod[:, sl, :].rearrange("p c r -> p (c r)"),
+                    scl[:, sl, :].rearrange("p c r -> p (c r)"),
+                    s1g[j][:, sl].rearrange("p c t r e -> p (c t r e)"),
+                )
+            first_stage(("s1", j // 2), j % 2, cod, scl)
+            if j % 2 == 1:
+                h_copy(4, j // 2, ("s1", j // 2))
+        h_quant(4)
+        second_stage(4, False, True)
+
+        for q in range(4):
+            if q % 2 == 0:
+                nc.scalar.activation(
+                    out=osb[:, q, :], in_=acc[q][:, 0:NW], func=ACT.Identity,
+                    bias=b2[:, q : q + 1], scale=0.125,
+                )
+            else:
+                nc.vector.tensor_scalar(
+                    out=osb[:, q, :], in0=acc[q][:, 0:NW], scalar1=0.125,
+                    scalar2=b2[:, q : q + 1], op0=ALU.mult, op1=ALU.add,
+                )
+            nc.sync.dma_start(out=outv[:, q], in_=osb[:, q, :].rearrange("p (b s) -> p b s", b=4))

@@ -3,8 +3,6 @@ from contextlib import ExitStack
 import concourse.mybir as mybir
 from concourse.masks import make_identity
 
-PIN = True
-
 FLOPS = 2 * 256 * 4096 * (512 + 2048) + 2 * 256 * 512 * (512 + 2048)
 
 BF16 = mybir.dt.bfloat16
@@ -20,29 +18,31 @@ NW = 256
 D = 4096
 NC = 8
 HALF = 2048
+NU = 16
 
 
 def tile_skconv2d_pa_kernel(tc, xw, S1s, U1s, U2s, S2s, bias, out):
     nc = tc.nc
     u2v = U2s.rearrange("t r k -> (t r) k").rearrange("(g p j) k -> p g j k", p=P, j=4)
-    s1v = S1s.rearrange("t (c p e) r -> p t c (e r)", c=NC, p=P, e=4)
+    s1v = S1s.rearrange("t (c p e) r -> p c t (e r)", c=NC, p=P, e=4)
     u1v = U1s.rearrange("t r o -> (t r) o").rearrange("(p j) o -> p j o", p=P)
     s2v = S2s.rearrange("t r o -> (t r) o").rearrange("(g p j) o -> p g j o", p=P, j=4)
     outv = out.rearrange("b (q p) i j -> p q b (i j)", p=P)
 
     with ExitStack() as ctx:
         const = ctx.enter_context(tc.tile_pool(name="const", bufs=1))
-        rawp = ctx.enter_context(tc.tile_pool(name="rawp", bufs=8))
+        rawp = ctx.enter_context(tc.tile_pool(name="rawp", bufs=9))
+        s1rp = ctx.enter_context(tc.tile_pool(name="s1rp", bufs=2))
+        wrp = ctx.enter_context(tc.tile_pool(name="wrp", bufs=3))
         grpp = ctx.enter_context(tc.tile_pool(name="grpp", bufs=3))
         codp = ctx.enter_context(tc.tile_pool(name="codp", bufs=3))
-        s1gp = ctx.enter_context(tc.tile_pool(name="s1gp", bufs=4))
+        s1gp = ctx.enter_context(tc.tile_pool(name="s1gp", bufs=2))
         s1cp = ctx.enter_context(tc.tile_pool(name="s1cp", bufs=4))
         wgp = ctx.enter_context(tc.tile_pool(name="wgp", bufs=2))
         hgp = ctx.enter_context(tc.tile_pool(name="hgp", bufs=2))
         tps = ctx.enter_context(tc.psum_pool(name="tps", bufs=6))
         hps = ctx.enter_context(tc.psum_pool(name="hps", bufs=2))
-        if PIN:
-            ctx.enter_context(tc.manual_schedule())
+        ctx.enter_context(tc.manual_schedule())
 
         ident_f = const.tile([P, P], F32, name="ident_f")
         make_identity(nc, ident_f[:])
@@ -54,8 +54,6 @@ def tile_skconv2d_pa_kernel(tc, xw, S1s, U1s, U2s, S2s, bias, out):
 
         xq = const.tile([P, NC, NW], U32, name="xq", align_bytes=64)
         xs = const.tile([P, NC, NW], U8, name="xs", align_bytes=64)
-        s2r = const.tile([P, 4, 4, 512], BF16, name="s2r")
-        u1r = const.tile([P, 4, 512], BF16, name="u1r")
         wc = const.tile([P, 5, 512], U32, name="wc", align_bytes=64)
         ws = const.tile([P, 5, 512], U8, name="ws", align_bytes=64)
         hqc = const.tile([P, 5, NW], U32, name="hqc", align_bytes=64)
@@ -72,29 +70,30 @@ def tile_skconv2d_pa_kernel(tc, xw, S1s, U1s, U2s, S2s, bias, out):
                 )
         u2raw = {}
         s1raw = {}
+        wraw = {}
+        w_items = [0, 1, 2, 4, 3]
 
-        def load_raw(n):
-            if n < 16:
-                t = rawp.tile([P, D], BF16, name="u2r", tag="raw")
-                nc.sync.dma_start(out=t[:], in_=u2v[:, n // 4, n % 4, :])
-                u2raw[n] = t
-            elif n < 20:
-                m = n - 16
-                t = rawp.tile([P, D], BF16, name="s1r", tag="raw")
-                for t2 in range(2):
-                    nc.sync.dma_start(
-                        out=t[:, HALF * t2 : HALF * (t2 + 1)].rearrange("p (c x) -> p c x", c=NC),
-                        in_=s1v[:, 2 * m + t2],
-                    )
-                s1raw[m] = t
-            if n == 3:
-                nc.sync.dma_start(out=u1r[:], in_=u1v)
-            if n in (5, 7, 9, 11):
-                g = (n - 5) // 2
-                nc.sync.dma_start(out=s2r[:, g], in_=s2v[:, g])
+        def load_s1(c):
+            if c % 2 == 0:
+                s1raw[c // 2] = s1rp.tile([P, 2, 8, 256], BF16, name="s1r", tag="s1r")
+            nc.sync.dma_start(out=s1raw[c // 2][:, c % 2], in_=s1v[:, c])
+
+        def load_w(s):
+            t = wrp.tile([P, 4, 512], BF16, name="wr", tag="wr")
+            nc.sync.dma_start(out=t[:], in_=u1v if s == 4 else s2v[:, s])
+            wraw[s] = t
+
+        def load(n):
+            t = rawp.tile([P, D], BF16, name="u2r", tag="raw")
+            nc.sync.dma_start(out=t[:], in_=u2v[:, n // 4, n % 4, :])
+            u2raw[n] = t
+            if 2 <= n < 10:
+                load_s1(n - 2)
+            elif 10 <= n < 15:
+                load_w(w_items[n - 10])
 
         for n in range(6):
-            load_raw(n)
+            load(n)
 
         def quant(codes, scales, src):
             nc.vector.quantize_mx(out=codes.bitcast(FP8X4), scales=scales, in_=src)
@@ -128,8 +127,8 @@ def tile_skconv2d_pa_kernel(tc, xw, S1s, U1s, U2s, S2s, bias, out):
             if c % 2 == 0 and c >= 2:
                 quant_x(c // 2 - 1)
         quant_x(3)
-        load_raw(6)
-        load_raw(7)
+        load(6)
+        load(7)
 
         bt = tps.tile([P, P], BF16, name="bt", tag="T")
         nc.tensor.transpose(bt[:], bz[:], ident_b[:])
@@ -139,6 +138,10 @@ def tile_skconv2d_pa_kernel(tc, xw, S1s, U1s, U2s, S2s, bias, out):
         u2cod = {}
         hbank = {}
         hgrp = {}
+        wgrp = {}
+        s1grp = {}
+        s1cod = {}
+        s1scl = {}
 
         def transposes(i):
             grp = grpp.tile([P, NC, P, 4], BF16, name="u2g", tag="grp", align_bytes=64)
@@ -158,12 +161,13 @@ def tile_skconv2d_pa_kernel(tc, xw, S1s, U1s, U2s, S2s, bias, out):
                     nc.vector.tensor_copy(out=gf[:, 2 * b : 2 * b + 2], in_=src)
                 else:
                     nc.scalar.copy(out=gf[:, 2 * b : 2 * b + 2], in_=src)
-            load_raw(8 + i)
+            if i + 8 < NU:
+                load(i + 8)
 
         def quant_u2(i):
             cod = codp.tile([P, NC, P], U32, name="u2c", tag="u2c", align_bytes=64)
             scl = codp.tile([P, NC, P], U8, name="u2s", tag="u2s", align_bytes=64)
-            u2cod[i] = (cod, scl)
+            u2cod[i] = [(cod[:, c, :], scl[:, c, :]) for c in range(NC)]
             for hf in range(2):
                 sl = slice(4 * hf, 4 * hf + 4)
                 quant(
@@ -172,15 +176,14 @@ def tile_skconv2d_pa_kernel(tc, xw, S1s, U1s, U2s, S2s, bias, out):
                     u2grp[i][:, sl].rearrange("p c r t -> p (c r t)"),
                 )
 
-        def first_stage(key, half, cod, scl):
+        def first_stage(key, half, weights):
             if half == 0:
                 hbank[key] = hps.tile([P, 2, NW], F32, name="hb", tag="h")
-            hb = hbank[key]
-            for c in range(NC):
+            for c, (cod, scl) in enumerate(weights):
                 nc.tensor.matmul_mx(
-                    out=hb[:, half, :],
-                    lhsT=cod[:, c, :].bitcast(FP8X4),
-                    lhsT_scale=scl[:, c, :],
+                    out=hbank[key][:, half, :],
+                    lhsT=cod.bitcast(FP8X4),
+                    lhsT_scale=scl,
                     rhs=xq[:, c, :].bitcast(FP8X4),
                     rhs_scale=xs[:, c, :],
                     start=(c == 0),
@@ -189,7 +192,7 @@ def tile_skconv2d_pa_kernel(tc, xw, S1s, U1s, U2s, S2s, bias, out):
 
         def h_copy(s, pair, key):
             if pair == 0:
-                hgrp[s] = hgp.tile([P, NW, 4], BF16, name="hg", tag="hg", align_bytes=64)
+                hgrp[s] = hgp.tile([P, NW, 4], BF16, name="hg", tag="hg%d" % (s // 4), align_bytes=64)
             nc.scalar.copy(
                 out=hgrp[s][:, :, 2 * pair : 2 * pair + 2],
                 in_=hbank[key][:].rearrange("p j n -> p n j"),
@@ -198,87 +201,94 @@ def tile_skconv2d_pa_kernel(tc, xw, S1s, U1s, U2s, S2s, bias, out):
         def h_quant(s):
             quant(hqc[:, s, :], hqs[:, s, :], hgrp[s][:].rearrange("p n t -> p (n t)"))
 
-        wgrp = {}
-
         def w_regroup(s):
-            wg = wgp.tile([P, 512, 4], BF16, name="wg", tag="wg", align_bytes=64)
-            wgrp[s] = wg
-            src = u1r[:] if s == 4 else s2r[:, s]
+            wgrp[s] = wgp.tile([P, 512, 4], BF16, name="wg", tag="wg", align_bytes=64)
             nc.vector.tensor_copy(
-                out=wg[:].rearrange("p (c i) t -> p c t i", i=4),
-                in_=src.rearrange("p t (c i) -> p c t i", i=4),
+                out=wgrp[s][:].rearrange("p (c i) t -> p c t i", i=4),
+                in_=wraw[s][:].rearrange("p t (c i) -> p c t i", i=4),
             )
 
         def w_quant(s):
             quant(wc[:, s, :], ws[:, s, :], wgrp[s][:].rearrange("p o t -> p (o t)"))
 
-        w_order = {4: 4, 6: 0, 8: 1, 10: 2, 12: 3}
+        def s1_regroup(k, j):
+            if j == 0:
+                s1grp[k] = s1gp.tile([P, 4, 2, P, 4], BF16, name="s1g", tag="s1g", align_bytes=64)
+            dst = s1grp[k][:, j].rearrange("p c (t r) e -> p (c t) r e", t=8)
+            src = s1raw[k][:].rearrange("p c t (e r j) -> p (c t) j r e", e=4, j=4)[:, :, j]
+            if j == 3:
+                nc.scalar.copy(out=dst, in_=src)
+            else:
+                nc.vector.tensor_copy(out=dst, in_=src)
 
-        transposes(0)
-        quant_u2(0)
-        transposes(1)
-        quant_u2(1)
-        for i in range(16):
+        def s1_quant(k, jj):
+            if jj == 0:
+                s1cod[k] = s1cp.tile([P, 4, 2, P], U32, name="s1c", tag="s1c", align_bytes=64)
+                s1scl[k] = s1cp.tile([P, 4, 2, P], U8, name="s1s", tag="s1s", align_bytes=64)
+            sl = slice(2 * jj, 2 * jj + 2)
+            quant(
+                s1cod[k][:, sl].rearrange("p j c r -> p (j c r)"),
+                s1scl[k][:, sl].rearrange("p j c r -> p (j c r)"),
+                s1grp[k][:, sl].rearrange("p j c r e -> p (j c r e)"),
+            )
+
+        def s1_weights(j):
+            return [
+                (s1cod[c // 2][:, j, c % 2, :], s1scl[c // 2][:, j, c % 2, :]) for c in range(NC)
+            ]
+
+        for n in range(2):
+            transposes(n)
+            quant_u2(n)
+        for i in range(NU):
             g, j = i // 4, i % 4
-            first_stage(("u2", i // 2), j % 2, u2cod[i][0], u2cod[i][1])
-            if i + 2 < 16:
-                transposes(i + 2)
+            first_stage(("u2", i // 2), j % 2, u2cod[i])
             if j % 2 == 1:
                 h_copy(g, j // 2, ("u2", i // 2))
-            if i + 2 < 16:
+            if 2 <= i < 10:
+                k = i // 2 - 1
+                if i % 2 == 0:
+                    s1_regroup(k, 0)
+                    s1_regroup(k, 1)
+                    s1_regroup(k, 3)
+                else:
+                    s1_regroup(k, 2)
+                    s1_quant(k, 0)
+                    s1_quant(k, 1)
+            if 10 <= i < 15:
+                w_regroup(w_items[i - 10])
+            if i == 14:
+                w_quant(3)
+            if i + 2 < NU:
+                transposes(i + 2)
                 quant_u2(i + 2)
+            if 10 <= i < 14:
+                w_quant(w_items[i - 10])
+                first_stage(("s1", (i - 10) // 2), i % 2, s1_weights(i - 10))
+            if i in (11, 13):
+                h_copy(4, (i - 10) // 2, ("s1", (i - 10) // 2))
             if j == 3:
                 h_quant(g)
-            if i in w_order:
-                w_regroup(w_order[i])
-            if i - 1 in w_order:
-                w_quant(w_order[i - 1])
+            if i == 13:
+                h_quant(4)
+            if i == 14:
+                acc = [tps.tile([P, 512], F32, name="acc%d" % q, tag="T") for q in range(4)]
 
-        acc = [tps.tile([P, 512], F32, name="acc%d" % q, tag="T") for q in range(4)]
+                def second_stage(s, start, stop):
+                    for q in range(4):
+                        nc.tensor.matmul_mx(
+                            out=acc[q][:, 0:NW],
+                            lhsT=wc[:, s, P * q : P * (q + 1)].bitcast(FP8X4),
+                            lhsT_scale=ws[:, s, P * q : P * (q + 1)],
+                            rhs=hqc[:, s, :].bitcast(FP8X4),
+                            rhs_scale=hqs[:, s, :],
+                            start=start,
+                            stop=stop,
+                        )
 
-        def second_stage(s, start, stop):
-            for q in range(4):
-                nc.tensor.matmul_mx(
-                    out=acc[q][:, 0:NW],
-                    lhsT=wc[:, s, P * q : P * (q + 1)].bitcast(FP8X4),
-                    lhsT_scale=ws[:, s, P * q : P * (q + 1)],
-                    rhs=hqc[:, s, :].bitcast(FP8X4),
-                    rhs_scale=hqs[:, s, :],
-                    start=start,
-                    stop=stop,
-                )
-
-        for g in range(4):
-            second_stage(g, g == 0, False)
-
-        s1g = [
-            s1gp.tile([P, NC, 8, 16, 4], BF16, name="s1g%d" % j, tag="s1g", align_bytes=64)
-            for j in range(4)
-        ]
-        for t in range(8):
-            src = s1raw[t // 2][:, HALF * (t % 2) : HALF * (t % 2 + 1)].rearrange(
-                "p (c e r j) -> p c j r e", c=NC, e=4, r=16, j=4
-            )
-            for j in range(4):
-                if j % 2 == 0:
-                    nc.vector.tensor_copy(out=s1g[j][:, :, t], in_=src[:, :, j])
-                else:
-                    nc.scalar.copy(out=s1g[j][:, :, t], in_=src[:, :, j])
-        for j in range(4):
-            cod = s1cp.tile([P, NC, P], U32, name="s1c", tag="s1c", align_bytes=64)
-            scl = s1cp.tile([P, NC, P], U8, name="s1s", tag="s1s", align_bytes=64)
-            for hf in range(2):
-                sl = slice(4 * hf, 4 * hf + 4)
-                quant(
-                    cod[:, sl, :].rearrange("p c r -> p (c r)"),
-                    scl[:, sl, :].rearrange("p c r -> p (c r)"),
-                    s1g[j][:, sl].rearrange("p c t r e -> p (c t r e)"),
-                )
-            first_stage(("s1", j // 2), j % 2, cod, scl)
-            if j % 2 == 1:
-                h_copy(4, j // 2, ("s1", j // 2))
-        h_quant(4)
-        second_stage(4, False, True)
+                for s in (0, 1, 2, 4):
+                    second_stage(s, s == 0, False)
+        second_stage(3, False, True)
 
         for q in range(4):
             if q % 2 == 0:

@@ -18,7 +18,9 @@ NW = 256
 D = 4096
 NC = 8
 HALF = 2048
+WSPLIT = 256
 NU = 16
+SORTED = range(11, 16)
 
 
 def tile_skconv2d_pa_kernel(tc, xw, S1s, U1s, U2s, S2s, bias, out):
@@ -31,15 +33,14 @@ def tile_skconv2d_pa_kernel(tc, xw, S1s, U1s, U2s, S2s, bias, out):
 
     with ExitStack() as ctx:
         const = ctx.enter_context(tc.tile_pool(name="const", bufs=1))
-        rawp = ctx.enter_context(tc.tile_pool(name="rawp", bufs=9))
-        s1rp = ctx.enter_context(tc.tile_pool(name="s1rp", bufs=2))
-        wrp = ctx.enter_context(tc.tile_pool(name="wrp", bufs=3))
+        rawp = ctx.enter_context(tc.tile_pool(name="rawp", bufs=8))
+        prmp = ctx.enter_context(tc.tile_pool(name="prmp", bufs=3))
+        s1rp = ctx.enter_context(tc.tile_pool(name="s1rp", bufs=3))
         grpp = ctx.enter_context(tc.tile_pool(name="grpp", bufs=3))
         codp = ctx.enter_context(tc.tile_pool(name="codp", bufs=3))
         s1gp = ctx.enter_context(tc.tile_pool(name="s1gp", bufs=2))
         s1cp = ctx.enter_context(tc.tile_pool(name="s1cp", bufs=4))
-        wgp = ctx.enter_context(tc.tile_pool(name="wgp", bufs=2))
-        hgp = ctx.enter_context(tc.tile_pool(name="hgp", bufs=2))
+        hgp = ctx.enter_context(tc.tile_pool(name="hgp", bufs=3))
         tps = ctx.enter_context(tc.psum_pool(name="tps", bufs=6))
         hps = ctx.enter_context(tc.psum_pool(name="hps", bufs=2))
         ctx.enter_context(tc.manual_schedule())
@@ -59,6 +60,7 @@ def tile_skconv2d_pa_kernel(tc, xw, S1s, U1s, U2s, S2s, bias, out):
         hqc = const.tile([P, 5, NW], U32, name="hqc", align_bytes=64)
         hqs = const.tile([P, 5, NW], U8, name="hqs", align_bytes=64)
         osb = const.tile([P, 4, NW], F32, name="osb")
+        psb = const.tile([P, 4, NW], F32, name="psb")
         b2 = const.tile([P, 4], F32, name="b2")
 
         xr = [rawp.tile([P, D], BF16, name="xr%d" % a, tag="raw") for a in range(2)]
@@ -71,29 +73,44 @@ def tile_skconv2d_pa_kernel(tc, xw, S1s, U1s, U2s, S2s, bias, out):
         u2raw = {}
         s1raw = {}
         wraw = {}
-        w_items = [0, 1, 2, 4, 3]
-
-        def load_s1(c):
-            if c % 2 == 0:
-                s1raw[c // 2] = s1rp.tile([P, 2, 8, 256], BF16, name="s1r", tag="s1r")
-            nc.sync.dma_start(out=s1raw[c // 2][:, c % 2], in_=s1v[:, c])
-
-        def load_w(s):
-            t = wrp.tile([P, 4, 512], BF16, name="wr", tag="wr")
-            nc.sync.dma_start(out=t[:], in_=u1v if s == 4 else s2v[:, s])
-            wraw[s] = t
-
-        def load(n):
-            t = rawp.tile([P, D], BF16, name="u2r", tag="raw")
-            nc.sync.dma_start(out=t[:], in_=u2v[:, n // 4, n % 4, :])
-            u2raw[n] = t
+        w_order = [0, 1, 2, 4, 3]
+        order = []
+        for n in range(NU):
+            order.append(("u", n))
             if 2 <= n < 10:
-                load_s1(n - 2)
+                order.append(("s", n - 2))
             elif 10 <= n < 15:
-                load_w(w_items[n - 10])
+                order.append(("w", w_order[n - 10]))
+        room = {"r": 8, "s": 6}
+        taken = {"r": 0, "s": 0}
+        issued = {"r": 2, "s": 0}
 
-        for n in range(6):
-            load(n)
+        def pump():
+            while order:
+                pool = "s" if order[0][0] == "s" else "r"
+                if issued[pool] - taken[pool] >= room[pool]:
+                    break
+                kind, n = order.pop(0)
+                issued[pool] += 1
+                if kind == "u":
+                    u2raw[n] = rawp.tile([P, D], BF16, name="u2r", tag="raw")
+                    parts = 2 if n == NU - 1 else 1
+                    for h in range(parts):
+                        ks = slice(D // parts * h, D // parts * (h + 1))
+                        nc.sync.dma_start(out=u2raw[n][:, ks], in_=u2v[:, n // 4, n % 4, ks])
+                elif kind == "s":
+                    if n % 2 == 0:
+                        s1raw[n // 2] = s1rp.tile([P, 2, 8, 256], BF16, name="s1r", tag="s1r")
+                    nc.sync.dma_start(out=s1raw[n // 2][:, n % 2], in_=s1v[:, n])
+                else:
+                    wraw[n] = rawp.tile([P, 4, 512], BF16, name="wr", tag="raw")
+                    nc.sync.dma_start(out=wraw[n][:], in_=u1v if n == 4 else s2v[:, n])
+
+        def read(kind, count=1):
+            taken[kind] += count
+            pump()
+
+        pump()
 
         def quant(codes, scales, src):
             nc.vector.quantize_mx(out=codes.bitcast(FP8X4), scales=scales, in_=src)
@@ -127,14 +144,14 @@ def tile_skconv2d_pa_kernel(tc, xw, S1s, U1s, U2s, S2s, bias, out):
             if c % 2 == 0 and c >= 2:
                 quant_x(c // 2 - 1)
         quant_x(3)
-        load(6)
-        load(7)
+        read("r", 2)
 
         bt = tps.tile([P, P], BF16, name="bt", tag="T")
         nc.tensor.transpose(bt[:], bz[:], ident_b[:])
         nc.scalar.mul(b2[:], bt[:, 0:4], 2.0)
 
         u2grp = {}
+        u2srt = {}
         u2cod = {}
         hbank = {}
         hgrp = {}
@@ -142,6 +159,19 @@ def tile_skconv2d_pa_kernel(tc, xw, S1s, U1s, U2s, S2s, bias, out):
         s1grp = {}
         s1cod = {}
         s1scl = {}
+
+        def sort_words(i):
+            u2srt[i] = []
+            for hf in range(2):
+                srt = prmp.tile([P, 4, 2, P], F32, name="srt", tag="srt")
+                u2srt[i].append(srt)
+                nc.vector.tensor_copy(
+                    out=srt[:],
+                    in_=u2raw[i][:].bitcast(F32)[:, 1024 * hf : 1024 * (hf + 1)].rearrange(
+                        "p (c r u) -> p c u r", c=4, u=2
+                    ),
+                )
+            read("r")
 
         def transposes(i):
             grp = grpp.tile([P, NC, P, 4], BF16, name="u2g", tag="grp", align_bytes=64)
@@ -153,16 +183,15 @@ def tile_skconv2d_pa_kernel(tc, xw, S1s, U1s, U2s, S2s, bias, out):
                 for c2 in range(2):
                     for u in range(2):
                         c = 2 * b + c2
-                        nc.tensor.transpose(
-                            bank[:, c2, u, :], rf[:, 256 * c + u : 256 * (c + 1) : 2], ident_f[:]
-                        )
+                        if i in SORTED:
+                            words = u2srt[i][c // 4][:, c % 4, u, :]
+                        else:
+                            words = rf[:, 256 * c + u : 256 * (c + 1) : 2]
+                        nc.tensor.transpose(bank[:, c2, u, :], words, ident_f[:])
                 src = bank[:].rearrange("p c u r -> p c r u")
-                if b == 0 and i % 2 == 1:
-                    nc.vector.tensor_copy(out=gf[:, 2 * b : 2 * b + 2], in_=src)
-                else:
-                    nc.scalar.copy(out=gf[:, 2 * b : 2 * b + 2], in_=src)
-            if i + 8 < NU:
-                load(i + 8)
+                nc.scalar.copy(out=gf[:, 2 * b : 2 * b + 2], in_=src)
+            if i not in SORTED:
+                read("r")
 
         def quant_u2(i):
             cod = codp.tile([P, NC, P], U32, name="u2c", tag="u2c", align_bytes=64)
@@ -178,7 +207,8 @@ def tile_skconv2d_pa_kernel(tc, xw, S1s, U1s, U2s, S2s, bias, out):
 
         def first_stage(key, half, weights):
             if half == 0:
-                hbank[key] = hps.tile([P, 2, NW], F32, name="hb", tag="h")
+                pool, tag = (hps, "h") if key[0] == "u2" else (tps, "T")
+                hbank[key] = pool.tile([P, 2, NW], F32, name="hb", tag=tag)
             for c, (cod, scl) in enumerate(weights):
                 nc.tensor.matmul_mx(
                     out=hbank[key][:, half, :],
@@ -192,7 +222,7 @@ def tile_skconv2d_pa_kernel(tc, xw, S1s, U1s, U2s, S2s, bias, out):
 
         def h_copy(s, pair, key):
             if pair == 0:
-                hgrp[s] = hgp.tile([P, NW, 4], BF16, name="hg", tag="hg%d" % (s // 4), align_bytes=64)
+                hgrp[s] = hgp.tile([P, NW, 4], BF16, name="hg", tag="hg", align_bytes=64)
             nc.scalar.copy(
                 out=hgrp[s][:, :, 2 * pair : 2 * pair + 2],
                 in_=hbank[key][:].rearrange("p j n -> p n j"),
@@ -202,11 +232,13 @@ def tile_skconv2d_pa_kernel(tc, xw, S1s, U1s, U2s, S2s, bias, out):
             quant(hqc[:, s, :], hqs[:, s, :], hgrp[s][:].rearrange("p n t -> p (n t)"))
 
         def w_regroup(s):
-            wgrp[s] = wgp.tile([P, 512, 4], BF16, name="wg", tag="wg", align_bytes=64)
-            nc.vector.tensor_copy(
-                out=wgrp[s][:].rearrange("p (c i) t -> p c t i", i=4),
-                in_=wraw[s][:].rearrange("p t (c i) -> p c t i", i=4),
-            )
+            wgrp[s] = s1gp.tile([P, 512, 4], BF16, name="wg", tag="s1g", align_bytes=64)
+            for eng, sl in ((nc.vector.tensor_copy, slice(0, WSPLIT)), (nc.scalar.copy, slice(WSPLIT, 512))):
+                eng(
+                    out=wgrp[s][:, sl].rearrange("p (c i) t -> p c t i", i=4),
+                    in_=wraw[s][:, :, sl].rearrange("p t (c i) -> p c t i", i=4),
+                )
+            read("r")
 
         def w_quant(s):
             quant(wc[:, s, :], ws[:, s, :], wgrp[s][:].rearrange("p o t -> p (o t)"))
@@ -220,6 +252,8 @@ def tile_skconv2d_pa_kernel(tc, xw, S1s, U1s, U2s, S2s, bias, out):
                 nc.scalar.copy(out=dst, in_=src)
             else:
                 nc.vector.tensor_copy(out=dst, in_=src)
+            if j == 2:
+                read("s", 2)
 
         def s1_quant(k, jj):
             if jj == 0:
@@ -237,68 +271,72 @@ def tile_skconv2d_pa_kernel(tc, xw, S1s, U1s, U2s, S2s, bias, out):
                 (s1cod[c // 2][:, j, c % 2, :], s1scl[c // 2][:, j, c % 2, :]) for c in range(NC)
             ]
 
+        def second_stage(parts, banks):
+            for q in range(4):
+                for n, s in enumerate(parts):
+                    nc.tensor.matmul_mx(
+                        out=banks[q // 2][:, q % 2, :],
+                        lhsT=wc[:, s, P * q : P * (q + 1)].bitcast(FP8X4),
+                        lhsT_scale=ws[:, s, P * q : P * (q + 1)],
+                        rhs=hqc[:, s, :].bitcast(FP8X4),
+                        rhs_scale=hqs[:, s, :],
+                        start=(n == 0),
+                        stop=(n == len(parts) - 1),
+                    )
+
+        def partial_sum():
+            banks = [tps.tile([P, 2, NW], F32, name="pb", tag="T") for _ in range(2)]
+            second_stage((0, 1, 2, 4), banks)
+            for q in range(4):
+                nc.scalar.activation(
+                    out=psb[:, q, :], in_=banks[q // 2][:, q % 2, :], func=ACT.Identity,
+                    bias=b2[:, q : q + 1], scale=0.125,
+                )
+
         for n in range(2):
             transposes(n)
             quant_u2(n)
         for i in range(NU):
             g, j = i // 4, i % 4
             first_stage(("u2", i // 2), j % 2, u2cod[i])
-            if j % 2 == 1:
-                h_copy(g, j // 2, ("u2", i // 2))
             if 2 <= i < 10:
                 k = i // 2 - 1
                 if i % 2 == 0:
-                    s1_regroup(k, 0)
-                    s1_regroup(k, 1)
-                    s1_regroup(k, 3)
+                    for jj in (0, 1, 3):
+                        s1_regroup(k, jj)
+                    s1_quant(k, 0)
                 else:
                     s1_regroup(k, 2)
-                    s1_quant(k, 0)
                     s1_quant(k, 1)
-            if 10 <= i < 15:
-                w_regroup(w_items[i - 10])
-            if i == 14:
-                w_quant(3)
+            elif i < 15:
+                if i >= 10:
+                    w_regroup(w_order[i - 10])
             if i + 2 < NU:
                 transposes(i + 2)
-                quant_u2(i + 2)
+            if j % 2 == 1:
+                h_copy(g, j // 2, ("u2", i // 2))
+            if i + 3 in SORTED:
+                sort_words(i + 3)
             if 10 <= i < 14:
-                w_quant(w_items[i - 10])
                 first_stage(("s1", (i - 10) // 2), i % 2, s1_weights(i - 10))
-            if i in (11, 13):
-                h_copy(4, (i - 10) // 2, ("s1", (i - 10) // 2))
+                if i % 2 == 1:
+                    h_copy(4, (i - 10) // 2, ("s1", (i - 10) // 2))
+                w_quant(w_order[i - 10])
+            if i == 15:
+                partial_sum()
+            if i + 2 < NU:
+                quant_u2(i + 2)
             if j == 3:
                 h_quant(g)
-            if i == 13:
-                h_quant(4)
             if i == 14:
-                acc = [tps.tile([P, 512], F32, name="acc%d" % q, tag="T") for q in range(4)]
+                h_quant(4)
+                w_quant(3)
 
-                def second_stage(s, start, stop):
-                    for q in range(4):
-                        nc.tensor.matmul_mx(
-                            out=acc[q][:, 0:NW],
-                            lhsT=wc[:, s, P * q : P * (q + 1)].bitcast(FP8X4),
-                            lhsT_scale=ws[:, s, P * q : P * (q + 1)],
-                            rhs=hqc[:, s, :].bitcast(FP8X4),
-                            rhs_scale=hqs[:, s, :],
-                            start=start,
-                            stop=stop,
-                        )
-
-                for s in (0, 1, 2, 4):
-                    second_stage(s, s == 0, False)
-        second_stage(3, False, True)
-
+        banks = [tps.tile([P, 2, NW], F32, name="fb", tag="T") for _ in range(2)]
+        second_stage((3,), banks)
         for q in range(4):
-            if q % 2 == 0:
-                nc.scalar.activation(
-                    out=osb[:, q, :], in_=acc[q][:, 0:NW], func=ACT.Identity,
-                    bias=b2[:, q : q + 1], scale=0.125,
-                )
-            else:
-                nc.vector.tensor_scalar(
-                    out=osb[:, q, :], in0=acc[q][:, 0:NW], scalar1=0.125,
-                    scalar2=b2[:, q : q + 1], op0=ALU.mult, op1=ALU.add,
-                )
+            nc.vector.scalar_tensor_tensor(
+                out=osb[:, q, :], in0=banks[q // 2][:, q % 2, :], scalar=0.125, in1=psb[:, q, :],
+                op0=ALU.mult, op1=ALU.add,
+            )
             nc.sync.dma_start(out=outv[:, q], in_=osb[:, q, :].rearrange("p (b s) -> p b s", b=4))

@@ -60,7 +60,6 @@ def tile_skconv2d_pa_kernel(tc, xw, S1s, U1s, U2s, S2s, bias, out):
         hqc = const.tile([P, 5, NW], U32, name="hqc", align_bytes=64)
         hqs = const.tile([P, 5, NW], U8, name="hqs", align_bytes=64)
         osb = const.tile([P, 4, NW], F32, name="osb")
-        psb = const.tile([P, 4, NW], F32, name="psb")
         b2 = const.tile([P, 4], F32, name="b2")
 
         xr = [rawp.tile([P, D], BF16, name="xr%d" % a, tag="raw") for a in range(2)]
@@ -271,27 +270,23 @@ def tile_skconv2d_pa_kernel(tc, xw, S1s, U1s, U2s, S2s, bias, out):
                 (s1cod[c // 2][:, j, c % 2, :], s1scl[c // 2][:, j, c % 2, :]) for c in range(NC)
             ]
 
-        def second_stage(parts, banks):
-            for q in range(4):
-                for n, s in enumerate(parts):
+        acc = []
+
+        def second_stage(parts):
+            if not acc:
+                for q in range(4):
+                    acc.append(tps.tile([P, NW], F32, name="acc", tag="T"))
+            for s in parts:
+                for q in range(4):
                     nc.tensor.matmul_mx(
-                        out=banks[q // 2][:, q % 2, :],
+                        out=acc[q][:],
                         lhsT=wc[:, s, P * q : P * (q + 1)].bitcast(FP8X4),
                         lhsT_scale=ws[:, s, P * q : P * (q + 1)],
                         rhs=hqc[:, s, :].bitcast(FP8X4),
                         rhs_scale=hqs[:, s, :],
-                        start=(n == 0),
-                        stop=(n == len(parts) - 1),
+                        start=(s == 0),
+                        stop=(s == 3),
                     )
-
-        def partial_sum():
-            banks = [tps.tile([P, 2, NW], F32, name="pb", tag="T") for _ in range(2)]
-            second_stage((0, 1, 2, 4), banks)
-            for q in range(4):
-                nc.scalar.activation(
-                    out=psb[:, q, :], in_=banks[q // 2][:, q % 2, :], func=ACT.Identity,
-                    bias=b2[:, q : q + 1], scale=0.125,
-                )
 
         for n in range(2):
             transposes(n)
@@ -323,7 +318,7 @@ def tile_skconv2d_pa_kernel(tc, xw, S1s, U1s, U2s, S2s, bias, out):
                     h_copy(4, (i - 10) // 2, ("s1", (i - 10) // 2))
                 w_quant(w_order[i - 10])
             if i == 15:
-                partial_sum()
+                second_stage((0, 1, 2, 4))
             if i + 2 < NU:
                 quant_u2(i + 2)
             if j == 3:
@@ -332,11 +327,16 @@ def tile_skconv2d_pa_kernel(tc, xw, S1s, U1s, U2s, S2s, bias, out):
                 h_quant(4)
                 w_quant(3)
 
-        banks = [tps.tile([P, 2, NW], F32, name="fb", tag="T") for _ in range(2)]
-        second_stage((3,), banks)
+        second_stage((3,))
         for q in range(4):
-            nc.vector.scalar_tensor_tensor(
-                out=osb[:, q, :], in0=banks[q // 2][:, q % 2, :], scalar=0.125, in1=psb[:, q, :],
-                op0=ALU.mult, op1=ALU.add,
-            )
+            if q % 2 == 0:
+                nc.scalar.activation(
+                    out=osb[:, q, :], in_=acc[q][:], func=ACT.Identity,
+                    bias=b2[:, q : q + 1], scale=0.125,
+                )
+            else:
+                nc.vector.tensor_scalar(
+                    out=osb[:, q, :], in0=acc[q][:], scalar1=0.125, scalar2=b2[:, q : q + 1],
+                    op0=ALU.mult, op1=ALU.add,
+                )
             nc.sync.dma_start(out=outv[:, q], in_=osb[:, q, :].rearrange("p (b s) -> p b s", b=4))

from contextlib import ExitStack

import concourse.mybir as mybir
from concourse.masks import make_identity

FLOPS = 2 * 256 * 4096 * (512 + 2048) + 2 * 256 * 512 * (512 + 2048)

BF16 = mybir.dt.bfloat16
F32 = mybir.dt.float32
U32 = mybir.dt.uint32
U8 = mybir.dt.uint8
FP8X4 = mybir.dt.float8_e4m3fn_x4
ACT = mybir.ActivationFunctionType
ALU = mybir.AluOpType

P = 128
NW = 256
D = 4096
NC = 8
HALF = 2048
WSPLIT = 256
NU = 16
SORTED = range(11, 16)


def tile_skconv2d_pa_kernel(tc, xw, S1s, U1s, U2s, S2s, bias, out):
    nc = tc.nc
    u2v = U2s.rearrange("t r k -> (t r) k").rearrange("(g p j) k -> p g j k", p=P, j=4)
    s1v = S1s.rearrange("t (c p e) r -> p c t (e r)", c=NC, p=P, e=4)
    u1v = U1s.rearrange("t r o -> (t r) o").rearrange("(p j) o -> p j o", p=P)
    s2v = S2s.rearrange("t r o -> (t r) o").rearrange("(g p j) o -> p g j o", p=P, j=4)
    outv = out.rearrange("b (q p) i j -> p q b (i j)", p=P)

    with ExitStack() as ctx:
        const = ctx.enter_context(tc.tile_pool(name="const", bufs=1))
        rawp = ctx.enter_context(tc.tile_pool(name="rawp", bufs=8))
        prmp = ctx.enter_context(tc.tile_pool(name="prmp", bufs=3))
        s1rp = ctx.enter_context(tc.tile_pool(name="s1rp", bufs=3))
        grpp = ctx.enter_context(tc.tile_pool(name="grpp", bufs=3))
        codp = ctx.enter_context(tc.tile_pool(name="codp", bufs=3))
        s1gp = ctx.enter_context(tc.tile_pool(name="s1gp", bufs=2))
        s1cp = ctx.enter_context(tc.tile_pool(name="s1cp", bufs=4))
        hgp = ctx.enter_context(tc.tile_pool(name="hgp", bufs=3))
        tps = ctx.enter_context(tc.psum_pool(name="tps", bufs=6))
        hps = ctx.enter_context(tc.psum_pool(name="hps", bufs=2))
        ctx.enter_context(tc.manual_schedule())

        ident_f = const.tile([P, P], F32, name="ident_f")
        make_identity(nc, ident_f[:])
        ident_b = const.tile([P, P], BF16, name="ident_b")
        make_identity(nc, ident_b[:])
        bz = const.tile([P, P], BF16, name="bz")
        nc.vector.memset(bz[:], 0.0)
        nc.scalar.dma_start(out=bz[0:4, :], in_=bias.rearrange("(a c) -> a c", a=4))

        xq = const.tile([P, NC, NW], U32, name="xq", align_bytes=64)
        xs = const.tile([P, NC, NW], U8, name="xs", align_bytes=64)
        wc = const.tile([P, 5, 512], U32, name="wc", align_bytes=64)
        ws = const.tile([P, 5, 512], U8, name="ws", align_bytes=64)
        hqc = const.tile([P, 5, NW], U32, name="hqc", align_bytes=64)
        hqs = const.tile([P, 5, NW], U8, name="hqs", align_bytes=64)
        osb = const.tile([P, 4, NW], F32, name="osb")
        b2 = const.tile([P, 4], F32, name="b2")

        xr = [rawp.tile([P, D], BF16, name="xr%d" % a, tag="raw") for a in range(2)]
        for hf in range(2):
            for a in range(2):
                nc.sync.dma_start(
                    out=xr[a][:, HALF * hf : HALF * (hf + 1)],
                    in_=xw[P * a : P * (a + 1), HALF * hf : HALF * (hf + 1)],
                )
        u2raw = {}
        s1raw = {}
        wraw = {}
        w_order = [0, 1, 2, 4, 3]
        order = []
        for n in range(NU):
            order.append(("u", n))
            if 2 <= n < 10:
                order.append(("s", n - 2))
            elif 10 <= n < 15:
                order.append(("w", w_order[n - 10]))
        room = {"r": 8, "s": 6}
        taken = {"r": 0, "s": 0}
        issued = {"r": 2, "s": 0}

        def pump():
            while order:
                pool = "s" if order[0][0] == "s" else "r"
                if issued[pool] - taken[pool] >= room[pool]:
                    break
                kind, n = order.pop(0)
                issued[pool] += 1
                if kind == "u":
                    u2raw[n] = rawp.tile([P, D], BF16, name="u2r", tag="raw")
                    parts = 2 if n == NU - 1 else 1
                    for h in range(parts):
                        ks = slice(D // parts * h, D // parts * (h + 1))
                        nc.sync.dma_start(out=u2raw[n][:, ks], in_=u2v[:, n // 4, n % 4, ks])
                elif kind == "s":
                    if n % 2 == 0:
                        s1raw[n // 2] = s1rp.tile([P, 2, 8, 256], BF16, name="s1r", tag="s1r")
                    nc.sync.dma_start(out=s1raw[n // 2][:, n % 2], in_=s1v[:, n])
                else:
                    wraw[n] = rawp.tile([P, 4, 512], BF16, name="wr", tag="raw")
                    nc.sync.dma_start(out=wraw[n][:], in_=u1v if n == 4 else s2v[:, n])

        def read(kind, count=1):
            taken[kind] += count
            pump()

        pump()

        def quant(codes, scales, src):
            nc.vector.quantize_mx(out=codes.bitcast(FP8X4), scales=scales, in_=src)

        xg = []

        def quant_x(k):
            quant(
                xq[:, 2 * k : 2 * k + 2, :].rearrange("p c n -> p (c n)"),
                xs[:, 2 * k : 2 * k + 2, :].rearrange("p c n -> p (c n)"),
                xg[k // 2][:, 2 * (k % 2) : 2 * (k % 2) + 2].rearrange("p c n t -> p (c n t)"),
            )

        for c in range(NC):
            if c % 4 == 0:
                xg.append(grpp.tile([P, 4, NW, 4], BF16, name="xg", tag="grp", align_bytes=64))
            gf = xg[c // 4][:].bitcast(F32)
            bank = tps.tile([P, 2, NW], F32, name="xb", tag="T")
            for u in range(2):
                for a in range(2):
                    nc.tensor.transpose(
                        bank[:, u, P * a : P * (a + 1)],
                        xr[a][:].bitcast(F32)[:, 256 * c + u : 256 * (c + 1) : 2],
                        ident_f[:],
                    )
            src = bank[:].rearrange("p u n -> p n u")
            if c % 2 == 0:
                nc.vector.tensor_copy(out=gf[:, c % 4], in_=src)
            else:
                nc.scalar.copy(out=gf[:, c % 4], in_=src)
            if c % 2 == 0 and c >= 2:
                quant_x(c // 2 - 1)
        quant_x(3)
        read("r", 2)

        bt = tps.tile([P, P], BF16, name="bt", tag="T")
        nc.tensor.transpose(bt[:], bz[:], ident_b[:])
        nc.scalar.mul(b2[:], bt[:, 0:4], 2.0)

        u2grp = {}
        u2srt = {}
        u2cod = {}
        hbank = {}
        hgrp = {}
        wgrp = {}
        s1grp = {}
        s1cod = {}
        s1scl = {}

        def sort_words(i):
            u2srt[i] = []
            for hf in range(2):
                srt = prmp.tile([P, 4, 2, P], F32, name="srt", tag="srt")
                u2srt[i].append(srt)
                nc.vector.tensor_copy(
                    out=srt[:],
                    in_=u2raw[i][:].bitcast(F32)[:, 1024 * hf : 1024 * (hf + 1)].rearrange(
                        "p (c r u) -> p c u r", c=4, u=2
                    ),
                )
            read("r")

        def transposes(i):
            grp = grpp.tile([P, NC, P, 4], BF16, name="u2g", tag="grp", align_bytes=64)
            u2grp[i] = grp
            gf = grp[:].bitcast(F32)
            rf = u2raw[i][:].bitcast(F32)
            for b in range(4):
                bank = tps.tile([P, 2, 2, P], F32, name="ub", tag="T")
                for c2 in range(2):
                    for u in range(2):
                        c = 2 * b + c2
                        if i in SORTED:
                            words = u2srt[i][c // 4][:, c % 4, u, :]
                        else:
                            words = rf[:, 256 * c + u : 256 * (c + 1) : 2]
                        nc.tensor.transpose(bank[:, c2, u, :], words, ident_f[:])
                src = bank[:].rearrange("p c u r -> p c r u")
                nc.scalar.copy(out=gf[:, 2 * b : 2 * b + 2], in_=src)
            if i not in SORTED:
                read("r")

        def quant_u2(i):
            cod = codp.tile([P, NC, P], U32, name="u2c", tag="u2c", align_bytes=64)
            scl = codp.tile([P, NC, P], U8, name="u2s", tag="u2s", align_bytes=64)
            u2cod[i] = [(cod[:, c, :], scl[:, c, :]) for c in range(NC)]
            for hf in range(2):
                sl = slice(4 * hf, 4 * hf + 4)
                quant(
                    cod[:, sl, :].rearrange("p c r -> p (c r)"),
                    scl[:, sl, :].rearrange("p c r -> p (c r)"),
                    u2grp[i][:, sl].rearrange("p c r t -> p (c r t)"),
                )

        def first_stage(key, half, weights):
            if half == 0:
                pool, tag = (hps, "h") if key[0] == "u2" else (tps, "T")
                hbank[key] = pool.tile([P, 2, NW], F32, name="hb", tag=tag)
            for c, (cod, scl) in enumerate(weights):
                nc.tensor.matmul_mx(
                    out=hbank[key][:, half, :],
                    lhsT=cod.bitcast(FP8X4),
                    lhsT_scale=scl,
                    rhs=xq[:, c, :].bitcast(FP8X4),
                    rhs_scale=xs[:, c, :],
                    start=(c == 0),
                    stop=(c == NC - 1),
                )

        def h_copy(s, pair, key):
            if pair == 0:
                hgrp[s] = hgp.tile([P, NW, 4], BF16, name="hg", tag="hg", align_bytes=64)
            nc.scalar.copy(
                out=hgrp[s][:, :, 2 * pair : 2 * pair + 2],
                in_=hbank[key][:].rearrange("p j n -> p n j"),
            )

        def h_quant(s):
            quant(hqc[:, s, :], hqs[:, s, :], hgrp[s][:].rearrange("p n t -> p (n t)"))

        def w_regroup(s):
            wgrp[s] = s1gp.tile([P, 512, 4], BF16, name="wg", tag="s1g", align_bytes=64)
            for eng, sl in ((nc.vector.tensor_copy, slice(0, WSPLIT)), (nc.scalar.copy, slice(WSPLIT, 512))):
                eng(
                    out=wgrp[s][:, sl].rearrange("p (c i) t -> p c t i", i=4),
                    in_=wraw[s][:, :, sl].rearrange("p t (c i) -> p c t i", i=4),
                )
            read("r")

        def w_quant(s):
            quant(wc[:, s, :], ws[:, s, :], wgrp[s][:].rearrange("p o t -> p (o t)"))

        def s1_regroup(k, j):
            if j == 0:
                s1grp[k] = s1gp.tile([P, 4, 2, P, 4], BF16, name="s1g", tag="s1g", align_bytes=64)
            dst = s1grp[k][:, j].rearrange("p c (t r) e -> p (c t) r e", t=8)
            src = s1raw[k][:].rearrange("p c t (e r j) -> p (c t) j r e", e=4, j=4)[:, :, j]
            if j == 3:
                nc.scalar.copy(out=dst, in_=src)
            else:
                nc.vector.tensor_copy(out=dst, in_=src)
            if j == 2:
                read("s", 2)

        def s1_quant(k, jj):
            if jj == 0:
                s1cod[k] = s1cp.tile([P, 4, 2, P], U32, name="s1c", tag="s1c", align_bytes=64)
                s1scl[k] = s1cp.tile([P, 4, 2, P], U8, name="s1s", tag="s1s", align_bytes=64)
            sl = slice(2 * jj, 2 * jj + 2)
            quant(
                s1cod[k][:, sl].rearrange("p j c r -> p (j c r)"),
                s1scl[k][:, sl].rearrange("p j c r -> p (j c r)"),
                s1grp[k][:, sl].rearrange("p j c r e -> p (j c r e)"),
            )

        def s1_weights(j):
            return [
                (s1cod[c // 2][:, j, c % 2, :], s1scl[c // 2][:, j, c % 2, :]) for c in range(NC)
            ]

        acc = []

        def second_stage(parts):
            if not acc:
                for q in range(4):
                    acc.append(tps.tile([P, NW], F32, name="acc", tag="T"))
            for s in parts:
                for q in range(4):
                    nc.tensor.matmul_mx(
                        out=acc[q][:],
                        lhsT=wc[:, s, P * q : P * (q + 1)].bitcast(FP8X4),
                        lhsT_scale=ws[:, s, P * q : P * (q + 1)],
                        rhs=hqc[:, s, :].bitcast(FP8X4),
                        rhs_scale=hqs[:, s, :],
                        start=(s == 0),
                        stop=(s == 3),
                    )

        for n in range(2):
            transposes(n)
            quant_u2(n)
        for i in range(NU):
            g, j = i // 4, i % 4
            first_stage(("u2", i // 2), j % 2, u2cod[i])
            if 2 <= i < 10:
                k = i // 2 - 1
                if i % 2 == 0:
                    for jj in (0, 1, 3):
                        s1_regroup(k, jj)
                    s1_quant(k, 0)
                else:
                    s1_regroup(k, 2)
                    s1_quant(k, 1)
            elif i < 15:
                if i >= 10:
                    w_regroup(w_order[i - 10])
            if i + 2 < NU:
                transposes(i + 2)
            if j % 2 == 1:
                h_copy(g, j // 2, ("u2", i // 2))
            if i + 3 in SORTED:
                sort_words(i + 3)
            if 10 <= i < 14:
                first_stage(("s1", (i - 10) // 2), i % 2, s1_weights(i - 10))
                if i % 2 == 1:
                    h_copy(4, (i - 10) // 2, ("s1", (i - 10) // 2))
                w_quant(w_order[i - 10])
            if i == 15:
                second_stage((0, 1, 2, 4))
            if i + 2 < NU:
                quant_u2(i + 2)
            if j == 3:
                h_quant(g)
            if i == 14:
                h_quant(4)
                w_quant(3)

        second_stage((3,))
        for q in range(4):
            if q % 2 == 0:
                nc.scalar.activation(
                    out=osb[:, q, :], in_=acc[q][:], func=ACT.Identity,
                    bias=b2[:, q : q + 1], scale=0.125,
                )
            else:
                nc.vector.tensor_scalar(
                    out=osb[:, q, :], in0=acc[q][:], scalar1=0.125, scalar2=b2[:, q : q + 1],
                    op0=ALU.mult, op1=ALU.add,
                )
            nc.sync.dma_start(out=outv[:, q], in_=osb[:, q, :].rearrange("p (b s) -> p b s", b=4))
